import numpy as np
import ml_dtypes


def mxq(x, axis, fmt="e4m3"):
    dtype, down = {"e4m3": (ml_dtypes.float8_e4m3fn, 7), "e5m2": (ml_dtypes.float8_e5m2, 14)}[fmt]
    v = np.moveaxis(np.asarray(x, np.float32).astype(ml_dtypes.bfloat16).astype(np.float64), axis, -1)
    blocks = v.reshape(v.shape[:-1] + (-1, 32))
    amax = np.abs(blocks).max(-1, keepdims=True)
    byte = np.maximum(np.where(amax > 0, np.frexp(amax)[1] - 1 + 127, 0) - down, 1)
    scale = np.exp2(byte - 127.0)
    codes = (blocks / scale).astype(np.float32).astype(dtype).astype(np.float64)
    return np.moveaxis((codes * scale).reshape(v.shape), -1, axis)


WIDE = False


def mx_kscale(k):
    if not WIDE:
        return np.ones(k)
    levels = np.array([10, -10, 5, -5, 0])
    a = np.random.permutation(np.resize(levels, k // 512 * 4)).reshape(k // 512, 4)
    idx = np.arange(k)
    return np.exp2(a[idx // 512, idx % 128 // 32])


BF16 = ml_dtypes.bfloat16


def bf(x):
    return np.asarray(x, np.float32).astype(BF16)


def f64(x):
    return np.asarray(x).astype(np.float64)


B, I, H, P = 512, 1024, 1024, 2048


def sigmoid(v):
    return 1.0 / (1.0 + np.exp(-v))


def setup_inputs():
    s = mx_kscale(H)
    s = s * np.exp2(-np.round(np.log2(s.mean())))
    return {"hidden_new": bf((1.6 + 1.5 * np.random.standard_normal((B, H))) * s),
            "persistent_memory": bf(0.2 * np.random.standard_normal((B, P))),
            "Waddr": bf(np.random.standard_normal((P, H)) * 3.0 / np.sqrt(H) / s[None, :]),
            "baddr": bf(np.random.standard_normal(P)),
            "Wwrite": bf(np.random.standard_normal((P, H)) * 0.7 / np.sqrt(H) / s[None, :]),
            "bwrite": bf(np.random.standard_normal(P)),
            "Wforget": bf(np.random.standard_normal((P, H)) * 0.7 / np.sqrt(H) / s[None, :]),
            "bforget": bf(1.0 + 0.3 * np.random.standard_normal(P))}


def reference(hidden_new, persistent_memory, Waddr, baddr, Wwrite, bwrite, Wforget, bforget):
    hn = f64(hidden_new)
    hq = mxq(hn, 1, "e4m3")
    z = (hq @ mxq(f64(Waddr), 1, "e4m3").T) + f64(baddr)
    e = np.exp(z - z.max(axis=1, keepdims=True))
    addr = e / e.sum(axis=1, keepdims=True)
    write = sigmoid((hq @ mxq(f64(Wwrite), 1, "e4m3").T) + f64(bwrite))
    forget = sigmoid((hq @ mxq(f64(Wforget), 1, "e4m3").T) + f64(bforget))
    hp = np.mean(hn, axis=1, keepdims=True)
    return forget * f64(persistent_memory) + write * hp * addr

@@ -1,0 +1,270 @@
+from contextlib import ExitStack
+
+import concourse.mybir as mybir
+from concourse.masks import make_identity
+
+F32 = mybir.dt.float32
+BF16 = mybir.dt.bfloat16
+U32 = mybir.dt.uint32
+U8 = mybir.dt.uint8
+FP8X4 = mybir.dt.float8_e4m3fn_x4
+ALU = mybir.AluOpType
+ACT = mybir.ActivationFunctionType
+AXIS = mybir.AxisListType
+
+P = 128
+BATCH = 512
+HIDDEN = 1024
+SLOTS = 2048
+PACK = 4
+PASSES = HIDDEN // (P * PACK)
+PAIRS = 2
+ROWS = 512
+ROW_TILES = ROWS // P
+ROW_WORDS = HIDDEN // 2
+BATCH_TILES = BATCH // P
+CHUNKS = SLOTS // ROWS
+SLOT_TILES = SLOTS // P
+RAW_BUFS = 6
+AHEAD = 2
+FORGET = 0
+WRITE = 1
+
+FLOPS = 2 * BATCH * HIDDEN * SLOTS * 3
+
+
+def tile_persistentgrucell_pc_kernel(
+    tc, hidden_new, persistent_memory, Waddr, baddr, Wwrite, bwrite, Wforget, bforget, out
+):
+    nc = tc.nc
+    with ExitStack() as stack:
+        const = stack.enter_context(tc.tile_pool(name="const", bufs=1))
+        raw_pool = stack.enter_context(tc.tile_pool(name="raw", bufs=RAW_BUFS))
+        grouped_pool = stack.enter_context(tc.tile_pool(name="grouped", bufs=3))
+        mx_pool = stack.enter_context(tc.tile_pool(name="mx", bufs=4))
+        score_pool = stack.enter_context(tc.tile_pool(name="score", bufs=2 * BATCH_TILES))
+        gate_pool = stack.enter_context(tc.tile_pool(name="gate", bufs=3))
+        kept_pool = stack.enter_context(tc.tile_pool(name="kept", bufs=2 * BATCH_TILES))
+        psum = stack.enter_context(tc.psum_pool(name="psum", bufs=8))
+
+        def chunk_rows(weight, c):
+            return weight[c * ROWS : (c + 1) * ROWS, :]
+
+        blocks = [chunk_rows(Waddr, c) for c in range(CHUNKS)]
+        for c in range(CHUNKS):
+            blocks.extend([chunk_rows(Wforget, c), chunk_rows(Wwrite, c)])
+        first_gate_block = CHUNKS
+
+        def load_rows(pool, rows):
+            raw_rows = pool.tile([P, ROW_TILES * HIDDEN], BF16, tag="raw")
+            nc.sync.dma_start(
+                out=raw_rows[:].rearrange("p (j k) -> p j k", j=ROW_TILES),
+                in_=rows.rearrange("(j p) k -> p j k", p=P),
+            )
+            return raw_rows
+
+        bias_rows = const.tile([P, P], BF16)
+        nc.vector.memset(bias_rows[:], 0.0)
+        for gate, bias in ((FORGET, bforget), (WRITE, bwrite)):
+            nc.sync.dma_start(
+                out=bias_rows[gate * SLOT_TILES : (gate + 1) * SLOT_TILES, :],
+                in_=bias.rearrange("(t p) -> t p", p=P),
+            )
+        hidden_raw = load_rows(const, hidden_new)
+        raw = {0: load_rows(raw_pool, blocks[0])}
+        baddr_all = const.tile([P, SLOTS], BF16)
+        nc.sync.dma_start(out=baddr_all[:], in_=baddr.partition_broadcast(P))
+        for n in range(1, RAW_BUFS):
+            raw[n] = load_rows(raw_pool, blocks[n])
+        memory = const.tile([P, BATCH_TILES, SLOTS], BF16)
+        nc.sync.dma_start(out=memory[:], in_=persistent_memory.rearrange("(i p) n -> p i n", p=P))
+
+        ident = const.tile([P, P], F32)
+        make_identity(nc, ident[:])
+
+        bias_rows_f32 = const.tile([P, P], F32)
+        nc.vector.tensor_copy(out=bias_rows_f32[:], in_=bias_rows[:])
+        bias_bank = psum.tile([P, P], F32, tag="bank")
+        nc.tensor.transpose(bias_bank[:], bias_rows_f32[:], ident[:])
+        gate_bias = const.tile([P, 2 * SLOT_TILES], F32)
+        nc.vector.tensor_copy(out=gate_bias[:], in_=bias_bank[:, 0 : 2 * SLOT_TILES])
+
+        def transpose_rows(raw_rows):
+            words = raw_rows[:].bitcast(F32)
+            grouped_rows = grouped_pool.tile([P, PASSES * ROWS * PACK], BF16, tag="grouped", align_bytes=64)
+            grouped_words = grouped_rows[:].bitcast(F32).rearrange("p (g r u) -> p g r u", g=PASSES, u=PAIRS)
+            for j in range(ROW_TILES):
+                bank = psum.tile([P, PASSES * PAIRS, P], F32, tag="bank")
+                for q in range(PASSES * PAIRS):
+                    first = j * ROW_WORDS + q * P
+                    nc.tensor.transpose(bank[:, q, :], words[:, first : first + P], ident[:])
+                nc.scalar.copy(
+                    out=grouped_words[:, :, j * P : (j + 1) * P, :],
+                    in_=bank[:].rearrange("p (g u) r -> p g r u", u=PAIRS),
+                )
+            return grouped_rows
+
+        def quantise(pool, grouped_rows):
+            codes = pool.tile([P, PASSES * ROWS], U32, tag="codes", align_bytes=64)
+            scales = pool.tile([P, PASSES * ROWS], U8, tag="scales", align_bytes=64)
+            nc.vector.quantize_mx(out=codes[:].bitcast(FP8X4), scales=scales[:], in_=grouped_rows[:])
+            return codes, scales
+
+        grouped = {}
+        mx = {}
+
+        def start_block(n):
+            if n < len(blocks):
+                grouped[n] = transpose_rows(raw[n])
+                if n + RAW_BUFS < len(blocks):
+                    raw[n + RAW_BUFS] = load_rows(raw_pool, blocks[n + RAW_BUFS])
+
+        def finish_block(n):
+            if n < len(blocks):
+                mx[n] = quantise(mx_pool, grouped[n])
+
+        def mx_product(acc, stationary, tile_index, moving):
+            for g in range(PASSES):
+                s_cols = slice(g * ROWS + tile_index * P, g * ROWS + (tile_index + 1) * P)
+                m_cols = slice(g * ROWS, (g + 1) * ROWS)
+                nc.tensor.matmul_mx(
+                    out=acc[:],
+                    lhsT=stationary[0][:, s_cols].bitcast(FP8X4),
+                    lhsT_scale=stationary[1][:, s_cols],
+                    rhs=moving[0][:, m_cols].bitcast(FP8X4),
+                    rhs_scale=moving[1][:, m_cols],
+                    start=(g == 0),
+                    stop=(g == PASSES - 1),
+                )
+
+        hidden_sum = const.tile([P, BATCH_TILES], F32)
+        hidden_rows = hidden_raw[:].rearrange("p (i k) -> p i k", i=BATCH_TILES)
+        half = BATCH_TILES // 2
+        nc.vector.tensor_reduce(out=hidden_sum[:, 0:half], in_=hidden_rows[:, 0:half, :], axis=AXIS.X, op=ALU.add)
+        hidden_mx = quantise(const, transpose_rows(hidden_raw))
+        nc.vector.tensor_reduce(
+            out=hidden_sum[:, half:BATCH_TILES], in_=hidden_rows[:, half:BATCH_TILES, :], axis=AXIS.X, op=ALU.add
+        )
+
+        exp_scores = const.tile([P, BATCH_TILES, SLOTS], F32)
+        neg_max = const.tile([P, BATCH_TILES, CHUNKS], F32)
+        exp_sum = const.tile([P, BATCH_TILES, CHUNKS], F32)
+
+        def scores_of(c):
+            cols = slice(c * ROWS, (c + 1) * ROWS)
+            scores = []
+            for i in range(BATCH_TILES):
+                acc = psum.tile([P, ROWS], F32, tag="bank")
+                mx_product(acc, hidden_mx, i, mx[c])
+                score = score_pool.tile([P, ROWS], F32, tag="score")
+                nc.vector.tensor_tensor(out=score[:], in0=acc[:], in1=baddr_all[:, cols], op=ALU.add)
+                scores.append(score)
+            return scores
+
+        def exponentials_of(c, scores):
+            cols = slice(c * ROWS, (c + 1) * ROWS)
+            for i in range(BATCH_TILES):
+                nc.vector.tensor_reduce(
+                    out=neg_max[:, i, c : c + 1], in_=scores[i][:], axis=AXIS.X, op=ALU.max, negate=True
+                )
+                nc.scalar.activation(
+                    out=exp_scores[:, i, cols],
+                    in_=scores[i][:],
+                    func=ACT.Exp,
+                    bias=neg_max[:, i, c : c + 1],
+                    scale=1.0,
+                    accum_out=exp_sum[:, i, c : c + 1],
+                )
+
+        for n in range(AHEAD):
+            start_block(n)
+            finish_block(n)
+        for c in range(CHUNKS):
+            scores = scores_of(c)
+            start_block(c + AHEAD)
+            exponentials_of(c, scores)
+            finish_block(c + AHEAD)
+
+        small = [P, BATCH_TILES, CHUNKS]
+        neg_top = const.tile([P, BATCH_TILES], F32)
+        nc.vector.tensor_reduce(out=neg_top[:], in_=neg_max[:], axis=AXIS.X, op=ALU.min)
+        below_top = const.tile(small, F32)
+        nc.vector.tensor_tensor(
+            out=below_top[:], in0=neg_top[:].unsqueeze(2).to_broadcast(small), in1=neg_max[:], op=ALU.subtract
+        )
+        rescale = const.tile(small, F32)
+        nc.scalar.activation(out=rescale[:], in_=below_top[:], func=ACT.Exp)
+        rescaled_sum = const.tile(small, F32)
+        nc.vector.tensor_tensor(out=rescaled_sum[:], in0=rescale[:], in1=exp_sum[:], op=ALU.mult)
+        row_sum = const.tile([P, BATCH_TILES], F32)
+        nc.vector.tensor_reduce(out=row_sum[:], in_=rescaled_sum[:], axis=AXIS.X, op=ALU.add)
+        inv_row_sum = const.tile([P, BATCH_TILES], F32)
+        nc.vector.reciprocal(out=inv_row_sum[:], in_=row_sum[:])
+        row_scale = const.tile([P, BATCH_TILES], F32)
+        nc.vector.scalar_tensor_tensor(
+            out=row_scale[:], in0=hidden_sum[:], scalar=1.0 / HIDDEN, in1=inv_row_sum[:], op0=ALU.mult, op1=ALU.mult
+        )
+        chunk_scale = const.tile(small, F32)
+        nc.vector.tensor_tensor(
+            out=chunk_scale[:], in0=rescale[:], in1=row_scale[:].unsqueeze(2).to_broadcast(small), op=ALU.mult
+        )
+
+        def gate_chunk(gate, c, weight_mx):
+            gate_t = gate_pool.tile([P, ROW_TILES, BATCH], F32, tag="gate")
+            for j in range(ROW_TILES):
+                acc = psum.tile([P, BATCH], F32, tag="bank")
+                mx_product(acc, weight_mx, j, hidden_mx)
+                col = gate * SLOT_TILES + c * ROW_TILES + j
+                nc.scalar.activation(
+                    out=gate_t[:, j, :], in_=acc[:], func=ACT.Sigmoid, bias=gate_bias[:, col : col + 1], scale=1.0
+                )
+            return gate_t
+
+        def batch_rows_of(gate_t, i):
+            bank = psum.tile([P, ROWS], F32, tag="bank")
+            for j in range(ROW_TILES):
+                nc.tensor.transpose(bank[:, j * P : (j + 1) * P], gate_t[:, j, i * P : (i + 1) * P], ident[:])
+            return bank
+
+        def keep_memory(c, forget_t):
+            cols = slice(c * ROWS, (c + 1) * ROWS)
+            kept = []
+            for i in range(BATCH_TILES):
+                bank = batch_rows_of(forget_t, i)
+                kept_i = kept_pool.tile([P, ROWS], F32, tag="kept")
+                nc.vector.tensor_tensor(out=kept_i[:], in0=bank[:], in1=memory[:, i, cols], op=ALU.mult)
+                kept.append(kept_i)
+            return kept
+
+        def add_written(c, write_t, kept):
+            cols = slice(c * ROWS, (c + 1) * ROWS)
+
+            def sum_and_store(i):
+                nc.vector.tensor_tensor(out=kept[i][:], in0=kept[i][:], in1=exp_scores[:, i, cols], op=ALU.add)
+                nc.sync.dma_start(out=out[i * P : (i + 1) * P, cols], in_=kept[i][:])
+
+            for i in range(BATCH_TILES):
+                bank = batch_rows_of(write_t, i)
+                nc.vector.scalar_tensor_tensor(
+                    out=exp_scores[:, i, cols],
+                    in0=exp_scores[:, i, cols],
+                    scalar=chunk_scale[:, i, c : c + 1],
+                    in1=bank[:],
+                    op0=ALU.mult,
+                    op1=ALU.mult,
+                )
+                if i > 0:
+                    sum_and_store(i - 1)
+            sum_and_store(BATCH_TILES - 1)
+
+        for c in range(CHUNKS):
+            forget_block = first_gate_block + 2 * c
+            write_block = forget_block + 1
+            forget_t = gate_chunk(FORGET, c, mx[forget_block])
+            start_block(forget_block + AHEAD)
+            kept = keep_memory(c, forget_t)
+            finish_block(forget_block + AHEAD)
+            write_t = gate_chunk(WRITE, c, mx[write_block])
+            start_block(write_block + AHEAD)
+            add_written(c, write_t, kept)
+            finish_block(write_block + AHEAD)

@@ -38,6 +38,7 @@ def tile_persistentgrucell_pc_kernel(
 ):
     nc = tc.nc
     with ExitStack() as stack:
+        stack.enter_context(tc.manual_schedule())
         const = stack.enter_context(tc.tile_pool(name="const", bufs=1))
         raw_pool = stack.enter_context(tc.tile_pool(name="raw", bufs=RAW_BUFS))
         grouped_pool = stack.enter_context(tc.tile_pool(name="grouped", bufs=3))

@@ -25,7 +25,7 @@ ROW_WORDS = HIDDEN // 2
 BATCH_TILES = BATCH // P
 CHUNKS = SLOTS // ROWS
 SLOT_TILES = SLOTS // P
-RAW_BUFS = 6
+RAW_BUFS = 5
 AHEAD = 2
 FORGET = 0
 WRITE = 1
@@ -41,54 +41,72 @@ def tile_persistentgrucell_pc_kernel(
         stack.enter_context(tc.manual_schedule())
         const = stack.enter_context(tc.tile_pool(name="const", bufs=1))
         raw_pool = stack.enter_context(tc.tile_pool(name="raw", bufs=RAW_BUFS))
-        grouped_pool = stack.enter_context(tc.tile_pool(name="grouped", bufs=3))
+        grouped_pool = stack.enter_context(tc.tile_pool(name="grouped", bufs=2))
         mx_pool = stack.enter_context(tc.tile_pool(name="mx", bufs=4))
         score_pool = stack.enter_context(tc.tile_pool(name="score", bufs=2 * BATCH_TILES))
         gate_pool = stack.enter_context(tc.tile_pool(name="gate", bufs=3))
-        kept_pool = stack.enter_context(tc.tile_pool(name="kept", bufs=2 * BATCH_TILES))
         psum = stack.enter_context(tc.psum_pool(name="psum", bufs=8))
 
         def chunk_rows(weight, c):
             return weight[c * ROWS : (c + 1) * ROWS, :]
 
-        blocks = [chunk_rows(Waddr, c) for c in range(CHUNKS)]
+        blocks = []
         for c in range(CHUNKS):
-            blocks.extend([chunk_rows(Wforget, c), chunk_rows(Wwrite, c)])
-        first_gate_block = CHUNKS
+            blocks.extend([chunk_rows(Waddr, c), chunk_rows(Wforget, c)])
+        first_write_block = len(blocks)
+        blocks.extend([chunk_rows(Wwrite, c) for c in range(CHUNKS)])
 
         def load_rows(pool, rows):
             raw_rows = pool.tile([P, ROW_TILES * HIDDEN], BF16, tag="raw")
-            nc.sync.dma_start(
-                out=raw_rows[:].rearrange("p (j k) -> p j k", j=ROW_TILES),
-                in_=rows.rearrange("(j p) k -> p j k", p=P),
-            )
+            for j in range(ROW_TILES):
+                nc.sync.dma_start(out=raw_rows[:, j * HIDDEN : (j + 1) * HIDDEN], in_=rows[j * P : (j + 1) * P, :])
             return raw_rows
 
+        ident = const.tile([P, P], F32)
+        make_identity(nc, ident[:])
+        ident_bf16 = const.tile([P, P], BF16)
+        make_identity(nc, ident_bf16[:])
+        ones = const.tile([P, P], BF16)
+        nc.vector.memset(ones[:], 1.0)
         bias_rows = const.tile([P, P], BF16)
         nc.vector.memset(bias_rows[:], 0.0)
+        baddr_row = const.tile([P, SLOTS], BF16)
+        nc.vector.memset(baddr_row[:], 0.0)
+
+        hidden_raw = load_rows(const, hidden_new)
+        raw = {0: load_rows(raw_pool, blocks[0])}
         for gate, bias in ((FORGET, bforget), (WRITE, bwrite)):
             nc.sync.dma_start(
                 out=bias_rows[gate * SLOT_TILES : (gate + 1) * SLOT_TILES, :],
                 in_=bias.rearrange("(t p) -> t p", p=P),
             )
-        hidden_raw = load_rows(const, hidden_new)
-        raw = {0: load_rows(raw_pool, blocks[0])}
-        baddr_all = const.tile([P, SLOTS], BF16)
-        nc.sync.dma_start(out=baddr_all[:], in_=baddr.partition_broadcast(P))
-        for n in range(1, RAW_BUFS):
+        nc.sync.dma_start(out=baddr_row[0:1, :], in_=baddr.rearrange("(o n) -> o n", o=1))
+        for n in range(1, AHEAD + 1):
             raw[n] = load_rows(raw_pool, blocks[n])
-        memory = const.tile([P, BATCH_TILES, SLOTS], BF16)
-        nc.sync.dma_start(out=memory[:], in_=persistent_memory.rearrange("(i p) n -> p i n", p=P))
+        half_memory = const.tile([P, BATCH_TILES, SLOTS], BF16)
+        nc.sync.dma_start(out=half_memory[:], in_=persistent_memory.rearrange("(i p) n -> p i n", p=P))
+        for n in range(AHEAD + 1, RAW_BUFS):
+            raw[n] = load_rows(raw_pool, blocks[n])
 
-        ident = const.tile([P, P], F32)
-        make_identity(nc, ident[:])
+        for c in range(CHUNKS):
+            cols = slice(c * ROWS, (c + 1) * ROWS)
+            nc.gpsimd.tensor_scalar(
+                out=half_memory[:, :, cols], in0=half_memory[:, :, cols], scalar1=0.5, scalar2=0.0, op0=ALU.mult, op1=ALU.add
+            )
 
-        bias_rows_f32 = const.tile([P, P], F32)
-        nc.vector.tensor_copy(out=bias_rows_f32[:], in_=bias_rows[:])
-        bias_bank = psum.tile([P, P], F32, tag="bank")
-        nc.tensor.transpose(bias_bank[:], bias_rows_f32[:], ident[:])
-        gate_bias = const.tile([P, 2 * SLOT_TILES], F32)
-        nc.vector.tensor_copy(out=gate_bias[:], in_=bias_bank[:, 0 : 2 * SLOT_TILES])
+        gate_bias = const.tile([P, 2, SLOT_TILES], F32)
+        baddr_all = const.tile([P, SLOTS], BF16)
+
+        def spread_biases():
+            bias_bank = psum.tile([P, P], BF16, tag="bank")
+            nc.tensor.transpose(bias_bank[:], bias_rows[:], ident_bf16[:])
+            nc.scalar.mul(out=gate_bias[:, FORGET, :], in_=bias_bank[:, 0:SLOT_TILES], mul=0.5)
+            nc.scalar.copy(out=gate_bias[:, WRITE, :], in_=bias_bank[:, SLOT_TILES : 2 * SLOT_TILES])
+            for c in range(CHUNKS):
+                cols = slice(c * ROWS, (c + 1) * ROWS)
+                baddr_bank = psum.tile([P, ROWS], F32, tag="bank")
+                nc.tensor.matmul(out=baddr_bank[:], lhsT=ones[:], rhs=baddr_row[:, cols], start=True, stop=True)
+                nc.scalar.copy(out=baddr_all[:, cols], in_=baddr_bank[:])
 
         def transpose_rows(raw_rows):
             words = raw_rows[:].bitcast(F32)
@@ -151,23 +169,26 @@ def tile_persistentgrucell_pc_kernel(
         neg_max = const.tile([P, BATCH_TILES, CHUNKS], F32)
         exp_sum = const.tile([P, BATCH_TILES, CHUNKS], F32)
 
-        def scores_of(c):
+        def scores_of(c, addr_mx):
             cols = slice(c * ROWS, (c + 1) * ROWS)
             scores = []
             for i in range(BATCH_TILES):
                 acc = psum.tile([P, ROWS], F32, tag="bank")
-                mx_product(acc, hidden_mx, i, mx[c])
+                mx_product(acc, hidden_mx, i, addr_mx)
                 score = score_pool.tile([P, ROWS], F32, tag="score")
                 nc.vector.tensor_tensor(out=score[:], in0=acc[:], in1=baddr_all[:, cols], op=ALU.add)
                 scores.append(score)
             return scores
 
-        def exponentials_of(c, scores):
-            cols = slice(c * ROWS, (c + 1) * ROWS)
+        def maxima_of(c, scores):
             for i in range(BATCH_TILES):
                 nc.vector.tensor_reduce(
                     out=neg_max[:, i, c : c + 1], in_=scores[i][:], axis=AXIS.X, op=ALU.max, negate=True
                 )
+
+        def exponentials_of(c, scores):
+            cols = slice(c * ROWS, (c + 1) * ROWS)
+            for i in range(BATCH_TILES):
                 nc.scalar.activation(
                     out=exp_scores[:, i, cols],
                     in_=scores[i][:],
@@ -177,14 +198,69 @@ def tile_persistentgrucell_pc_kernel(
                     accum_out=exp_sum[:, i, c : c + 1],
                 )
 
-        for n in range(AHEAD):
-            start_block(n)
-            finish_block(n)
+        def gate_chunk(gate, c, weight_mx, func, scale):
+            gate_t = gate_pool.tile([P, ROW_TILES, BATCH], F32, tag="gate")
+            for j in range(ROW_TILES):
+                acc = psum.tile([P, BATCH], F32, tag="bank")
+                mx_product(acc, weight_mx, j, hidden_mx)
+                t = c * ROW_TILES + j
+                nc.scalar.activation(
+                    out=gate_t[:, j, :], in_=acc[:], func=func, bias=gate_bias[:, gate, t : t + 1], scale=scale
+                )
+            return gate_t
+
+        def batch_rows_of(gate_t, i):
+            bank = psum.tile([P, ROWS], F32, tag="bank")
+            for j in range(ROW_TILES):
+                nc.tensor.transpose(bank[:, j * P : (j + 1) * P], gate_t[:, j, i * P : (i + 1) * P], ident[:])
+            return bank
+
+        result = const.tile([P, BATCH_TILES, SLOTS], F32)
+
+        def keep_memory(c, tanh_t):
+            cols = slice(c * ROWS, (c + 1) * ROWS)
+            for i in range(BATCH_TILES):
+                bank = batch_rows_of(tanh_t, i)
+                nc.vector.scalar_tensor_tensor(
+                    out=result[:, i, cols], in0=bank[:], scalar=1.0, in1=half_memory[:, i, cols], op0=ALU.add, op1=ALU.mult
+                )
+
+        def add_written(c, write_t):
+            cols = slice(c * ROWS, (c + 1) * ROWS)
+            for i in range(BATCH_TILES):
+                bank = batch_rows_of(write_t, i)
+                nc.vector.scalar_tensor_tensor(
+                    out=exp_scores[:, i, cols],
+                    in0=exp_scores[:, i, cols],
+                    scalar=chunk_scale[:, i, c : c + 1],
+                    in1=bank[:],
+                    op0=ALU.mult,
+                    op1=ALU.mult,
+                )
+                adder = (nc.gpsimd, nc.vector)[i % 2]
+                adder.tensor_tensor(
+                    out=result[:, i, cols], in0=result[:, i, cols], in1=exp_scores[:, i, cols], op=ALU.add
+                )
+                nc.sync.dma_start(out=out[i * P : (i + 1) * P, cols], in_=result[:, i, cols])
+
+        start_block(0)
+        finish_block(0)
+        spread_biases()
+        start_block(1)
+        finish_block(1)
+
         for c in range(CHUNKS):
-            scores = scores_of(c)
-            start_block(c + AHEAD)
+            addr_block = 2 * c
+            forget_block = addr_block + 1
+            scores = scores_of(c, mx[addr_block])
+            start_block(addr_block + AHEAD)
+            maxima_of(c, scores)
+            finish_block(addr_block + AHEAD)
+            tanh_t = gate_chunk(FORGET, c, mx[forget_block], ACT.Tanh, 0.5)
+            start_block(forget_block + AHEAD)
             exponentials_of(c, scores)
-            finish_block(c + AHEAD)
+            keep_memory(c, tanh_t)
+            finish_block(forget_block + AHEAD)
 
         small = [P, BATCH_TILES, CHUNKS]
         neg_top = const.tile([P, BATCH_TILES], F32)
@@ -210,62 +286,9 @@ def tile_persistentgrucell_pc_kernel(
             out=chunk_scale[:], in0=rescale[:], in1=row_scale[:].unsqueeze(2).to_broadcast(small), op=ALU.mult
         )
 
-        def gate_chunk(gate, c, weight_mx):
-            gate_t = gate_pool.tile([P, ROW_TILES, BATCH], F32, tag="gate")
-            for j in range(ROW_TILES):
-                acc = psum.tile([P, BATCH], F32, tag="bank")
-                mx_product(acc, weight_mx, j, hidden_mx)
-                col = gate * SLOT_TILES + c * ROW_TILES + j
-                nc.scalar.activation(
-                    out=gate_t[:, j, :], in_=acc[:], func=ACT.Sigmoid, bias=gate_bias[:, col : col + 1], scale=1.0
-                )
-            return gate_t
-
-        def batch_rows_of(gate_t, i):
-            bank = psum.tile([P, ROWS], F32, tag="bank")
-            for j in range(ROW_TILES):
-                nc.tensor.transpose(bank[:, j * P : (j + 1) * P], gate_t[:, j, i * P : (i + 1) * P], ident[:])
-            return bank
-
-        def keep_memory(c, forget_t):
-            cols = slice(c * ROWS, (c + 1) * ROWS)
-            kept = []
-            for i in range(BATCH_TILES):
-                bank = batch_rows_of(forget_t, i)
-                kept_i = kept_pool.tile([P, ROWS], F32, tag="kept")
-                nc.vector.tensor_tensor(out=kept_i[:], in0=bank[:], in1=memory[:, i, cols], op=ALU.mult)
-                kept.append(kept_i)
-            return kept
-
-        def add_written(c, write_t, kept):
-            cols = slice(c * ROWS, (c + 1) * ROWS)
-
-            def sum_and_store(i):
-                nc.vector.tensor_tensor(out=kept[i][:], in0=kept[i][:], in1=exp_scores[:, i, cols], op=ALU.add)
-                nc.sync.dma_start(out=out[i * P : (i + 1) * P, cols], in_=kept[i][:])
-
-            for i in range(BATCH_TILES):
-                bank = batch_rows_of(write_t, i)
-                nc.vector.scalar_tensor_tensor(
-                    out=exp_scores[:, i, cols],
-                    in0=exp_scores[:, i, cols],
-                    scalar=chunk_scale[:, i, c : c + 1],
-                    in1=bank[:],
-                    op0=ALU.mult,
-                    op1=ALU.mult,
-                )
-                if i > 0:
-                    sum_and_store(i - 1)
-            sum_and_store(BATCH_TILES - 1)
-
         for c in range(CHUNKS):
-            forget_block = first_gate_block + 2 * c
-            write_block = forget_block + 1
-            forget_t = gate_chunk(FORGET, c, mx[forget_block])
-            start_block(forget_block + AHEAD)
-            kept = keep_memory(c, forget_t)
-            finish_block(forget_block + AHEAD)
-            write_t = gate_chunk(WRITE, c, mx[write_block])
+            write_block = first_write_block + c
+            write_t = gate_chunk(WRITE, c, mx[write_block], ACT.Sigmoid, 1.0)
             start_block(write_block + AHEAD)
-            add_written(c, write_t, kept)
+            add_written(c, write_t)
             finish_block(write_block + AHEAD)

@@ -27,6 +27,7 @@ CHUNKS = SLOTS // ROWS
 SLOT_TILES = SLOTS // P
 RAW_BUFS = 5
 AHEAD = 2
+GATE_RUN = 2
 FORGET = 0
 WRITE = 1
 
@@ -198,16 +199,14 @@ def tile_persistentgrucell_pc_kernel(
                     accum_out=exp_sum[:, i, c : c + 1],
                 )
 
-        def gate_chunk(gate, c, weight_mx, func, scale):
-            gate_t = gate_pool.tile([P, ROW_TILES, BATCH], F32, tag="gate")
-            for j in range(ROW_TILES):
+        def gate_tiles(gate_t, run, gate, c, weight_mx, func, scale):
+            for j in range(run * GATE_RUN, (run + 1) * GATE_RUN):
                 acc = psum.tile([P, BATCH], F32, tag="bank")
                 mx_product(acc, weight_mx, j, hidden_mx)
                 t = c * ROW_TILES + j
                 nc.scalar.activation(
                     out=gate_t[:, j, :], in_=acc[:], func=func, bias=gate_bias[:, gate, t : t + 1], scale=scale
                 )
-            return gate_t
 
         def batch_rows_of(gate_t, i):
             bank = psum.tile([P, ROWS], F32, tag="bank")
@@ -254,12 +253,16 @@ def tile_persistentgrucell_pc_kernel(
             forget_block = addr_block + 1
             scores = scores_of(c, mx[addr_block])
             start_block(addr_block + AHEAD)
-            maxima_of(c, scores)
             finish_block(addr_block + AHEAD)
-            tanh_t = gate_chunk(FORGET, c, mx[forget_block], ACT.Tanh, 0.5)
+            earlier_tanh_t = tanh_t if c > 0 else None
+            tanh_t = gate_pool.tile([P, ROW_TILES, BATCH], F32, tag="gate")
+            gate_tiles(tanh_t, 0, FORGET, c, mx[forget_block], ACT.Tanh, 0.5)
+            if c > 0:
+                keep_memory(c - 1, earlier_tanh_t)
+            gate_tiles(tanh_t, 1, FORGET, c, mx[forget_block], ACT.Tanh, 0.5)
             start_block(forget_block + AHEAD)
+            maxima_of(c, scores)
             exponentials_of(c, scores)
-            keep_memory(c, tanh_t)
             finish_block(forget_block + AHEAD)
 
         small = [P, BATCH_TILES, CHUNKS]
@@ -288,7 +291,14 @@ def tile_persistentgrucell_pc_kernel(
 
         for c in range(CHUNKS):
             write_block = first_write_block + c
-            write_t = gate_chunk(WRITE, c, mx[write_block], ACT.Sigmoid, 1.0)
+            earlier_write_t = write_t if c > 0 else None
+            write_t = gate_pool.tile([P, ROW_TILES, BATCH], F32, tag="gate")
+            gate_tiles(write_t, 0, WRITE, c, mx[write_block], ACT.Sigmoid, 1.0)
+            if c > 0:
+                add_written(c - 1, earlier_write_t)
+            else:
+                keep_memory(CHUNKS - 1, tanh_t)
+            gate_tiles(write_t, 1, WRITE, c, mx[write_block], ACT.Sigmoid, 1.0)
             start_block(write_block + AHEAD)
-            add_written(c, write_t)
             finish_block(write_block + AHEAD)
+        add_written(CHUNKS - 1, write_t)

@@ -25,11 +25,8 @@ ROW_WORDS = HIDDEN // 2
 BATCH_TILES = BATCH // P
 CHUNKS = SLOTS // ROWS
 SLOT_TILES = SLOTS // P
-RAW_BUFS = 5
+RAW_BUFS = 4
 AHEAD = 2
-GATE_RUN = 2
-FORGET = 0
-WRITE = 1
 
 FLOPS = 2 * BATCH * HIDDEN * SLOTS * 3
 
@@ -44,8 +41,8 @@ def tile_persistentgrucell_pc_kernel(
         raw_pool = stack.enter_context(tc.tile_pool(name="raw", bufs=RAW_BUFS))
         grouped_pool = stack.enter_context(tc.tile_pool(name="grouped", bufs=2))
         mx_pool = stack.enter_context(tc.tile_pool(name="mx", bufs=4))
-        score_pool = stack.enter_context(tc.tile_pool(name="score", bufs=2 * BATCH_TILES))
-        gate_pool = stack.enter_context(tc.tile_pool(name="gate", bufs=3))
+        affine_pool = stack.enter_context(tc.tile_pool(name="affine", bufs=3 * BATCH_TILES))
+        gate_pool = stack.enter_context(tc.tile_pool(name="gate", bufs=2))
         psum = stack.enter_context(tc.psum_pool(name="psum", bufs=8))
 
         def chunk_rows(weight, c):
@@ -69,45 +66,29 @@ def tile_persistentgrucell_pc_kernel(
         make_identity(nc, ident_bf16[:])
         ones = const.tile([P, P], BF16)
         nc.vector.memset(ones[:], 1.0)
-        bias_rows = const.tile([P, P], BF16)
-        nc.vector.memset(bias_rows[:], 0.0)
+        bwrite_rows = const.tile([P, P], BF16)
+        nc.vector.memset(bwrite_rows[:], 0.0)
         baddr_row = const.tile([P, SLOTS], BF16)
         nc.vector.memset(baddr_row[:], 0.0)
+        bforget_row = const.tile([P, SLOTS], BF16)
+        nc.vector.memset(bforget_row[:], 0.0)
 
         hidden_raw = load_rows(const, hidden_new)
         raw = {0: load_rows(raw_pool, blocks[0])}
-        for gate, bias in ((FORGET, bforget), (WRITE, bwrite)):
-            nc.sync.dma_start(
-                out=bias_rows[gate * SLOT_TILES : (gate + 1) * SLOT_TILES, :],
-                in_=bias.rearrange("(t p) -> t p", p=P),
-            )
         nc.sync.dma_start(out=baddr_row[0:1, :], in_=baddr.rearrange("(o n) -> o n", o=1))
-        for n in range(1, AHEAD + 1):
+        nc.sync.dma_start(out=bforget_row[0:1, :], in_=bforget.rearrange("(o n) -> o n", o=1))
+        nc.sync.dma_start(out=bwrite_rows[0:SLOT_TILES, :], in_=bwrite.rearrange("(t p) -> t p", p=P))
+        for n in range(1, RAW_BUFS):
             raw[n] = load_rows(raw_pool, blocks[n])
-        half_memory = const.tile([P, BATCH_TILES, SLOTS], BF16)
-        nc.sync.dma_start(out=half_memory[:], in_=persistent_memory.rearrange("(i p) n -> p i n", p=P))
-        for n in range(AHEAD + 1, RAW_BUFS):
-            raw[n] = load_rows(raw_pool, blocks[n])
+        memory = const.tile([P, BATCH_TILES, SLOTS], BF16)
+        nc.sync.dma_start(out=memory[:], in_=persistent_memory.rearrange("(i p) n -> p i n", p=P))
 
-        for c in range(CHUNKS):
-            cols = slice(c * ROWS, (c + 1) * ROWS)
-            nc.gpsimd.tensor_scalar(
-                out=half_memory[:, :, cols], in0=half_memory[:, :, cols], scalar1=0.5, scalar2=0.0, op0=ALU.mult, op1=ALU.add
-            )
-
-        gate_bias = const.tile([P, 2, SLOT_TILES], F32)
-        baddr_all = const.tile([P, SLOTS], BF16)
-
-        def spread_biases():
-            bias_bank = psum.tile([P, P], BF16, tag="bank")
-            nc.tensor.transpose(bias_bank[:], bias_rows[:], ident_bf16[:])
-            nc.scalar.mul(out=gate_bias[:, FORGET, :], in_=bias_bank[:, 0:SLOT_TILES], mul=0.5)
-            nc.scalar.copy(out=gate_bias[:, WRITE, :], in_=bias_bank[:, SLOT_TILES : 2 * SLOT_TILES])
+        def spread_over_partitions(bias_row, bias_all, copy_out):
             for c in range(CHUNKS):
                 cols = slice(c * ROWS, (c + 1) * ROWS)
-                baddr_bank = psum.tile([P, ROWS], F32, tag="bank")
-                nc.tensor.matmul(out=baddr_bank[:], lhsT=ones[:], rhs=baddr_row[:, cols], start=True, stop=True)
-                nc.scalar.copy(out=baddr_all[:, cols], in_=baddr_bank[:])
+                bias_bank = psum.tile([P, ROWS], F32, tag="bank")
+                nc.tensor.matmul(out=bias_bank[:], lhsT=ones[:], rhs=bias_row[:, cols], start=True, stop=True)
+                copy_out(out=bias_all[:, cols], in_=bias_bank[:])
 
         def transpose_rows(raw_rows):
             words = raw_rows[:].bitcast(F32)
@@ -166,20 +147,20 @@ def tile_persistentgrucell_pc_kernel(
             out=hidden_sum[:, half:BATCH_TILES], in_=hidden_rows[:, half:BATCH_TILES, :], axis=AXIS.X, op=ALU.add
         )
 
+        def affine_of(c, weight_mx, bias_all):
+            cols = slice(c * ROWS, (c + 1) * ROWS)
+            tiles = []
+            for i in range(BATCH_TILES):
+                acc = psum.tile([P, ROWS], F32, tag="bank")
+                mx_product(acc, hidden_mx, i, weight_mx)
+                affine = affine_pool.tile([P, ROWS], F32, tag="affine")
+                nc.vector.tensor_tensor(out=affine[:], in0=acc[:], in1=bias_all[:, cols], op=ALU.add)
+                tiles.append(affine)
+            return tiles
+
         exp_scores = const.tile([P, BATCH_TILES, SLOTS], F32)
         neg_max = const.tile([P, BATCH_TILES, CHUNKS], F32)
         exp_sum = const.tile([P, BATCH_TILES, CHUNKS], F32)
-
-        def scores_of(c, addr_mx):
-            cols = slice(c * ROWS, (c + 1) * ROWS)
-            scores = []
-            for i in range(BATCH_TILES):
-                acc = psum.tile([P, ROWS], F32, tag="bank")
-                mx_product(acc, hidden_mx, i, addr_mx)
-                score = score_pool.tile([P, ROWS], F32, tag="score")
-                nc.vector.tensor_tensor(out=score[:], in0=acc[:], in1=baddr_all[:, cols], op=ALU.add)
-                scores.append(score)
-            return scores
 
         def maxima_of(c, scores):
             for i in range(BATCH_TILES):
@@ -199,35 +180,36 @@ def tile_persistentgrucell_pc_kernel(
                     accum_out=exp_sum[:, i, c : c + 1],
                 )
 
-        def gate_tiles(gate_t, run, gate, c, weight_mx, func, scale):
-            for j in range(run * GATE_RUN, (run + 1) * GATE_RUN):
+        result = const.tile([P, BATCH_TILES, SLOTS], F32)
+
+        def keep_memory(c, forget):
+            cols = slice(c * ROWS, (c + 1) * ROWS)
+            for i in range(BATCH_TILES):
+                nc.scalar.activation(out=forget[i][:], in_=forget[i][:], func=ACT.Tanh, scale=0.5)
+                nc.gpsimd.tensor_scalar(
+                    out=forget[i][:], in0=forget[i][:], scalar1=0.5, scalar2=0.5, op0=ALU.mult, op1=ALU.add
+                )
+                nc.gpsimd.tensor_tensor(out=result[:, i, cols], in0=forget[i][:], in1=memory[:, i, cols], op=ALU.mult)
+
+        bwrite_cols = const.tile([P, SLOT_TILES], F32)
+
+        def write_chunk(c, weight_mx):
+            write_t = gate_pool.tile([P, ROW_TILES, BATCH], F32, tag="gate")
+            for j in range(ROW_TILES):
                 acc = psum.tile([P, BATCH], F32, tag="bank")
                 mx_product(acc, weight_mx, j, hidden_mx)
                 t = c * ROW_TILES + j
                 nc.scalar.activation(
-                    out=gate_t[:, j, :], in_=acc[:], func=func, bias=gate_bias[:, gate, t : t + 1], scale=scale
+                    out=write_t[:, j, :], in_=acc[:], func=ACT.Sigmoid, bias=bwrite_cols[:, t : t + 1], scale=1.0
                 )
-
-        def batch_rows_of(gate_t, i):
-            bank = psum.tile([P, ROWS], F32, tag="bank")
-            for j in range(ROW_TILES):
-                nc.tensor.transpose(bank[:, j * P : (j + 1) * P], gate_t[:, j, i * P : (i + 1) * P], ident[:])
-            return bank
-
-        result = const.tile([P, BATCH_TILES, SLOTS], F32)
-
-        def keep_memory(c, tanh_t):
-            cols = slice(c * ROWS, (c + 1) * ROWS)
-            for i in range(BATCH_TILES):
-                bank = batch_rows_of(tanh_t, i)
-                nc.vector.scalar_tensor_tensor(
-                    out=result[:, i, cols], in0=bank[:], scalar=1.0, in1=half_memory[:, i, cols], op0=ALU.add, op1=ALU.mult
-                )
+            return write_t
 
         def add_written(c, write_t):
             cols = slice(c * ROWS, (c + 1) * ROWS)
             for i in range(BATCH_TILES):
-                bank = batch_rows_of(write_t, i)
+                bank = psum.tile([P, ROWS], F32, tag="bank")
+                for j in range(ROW_TILES):
+                    nc.tensor.transpose(bank[:, j * P : (j + 1) * P], write_t[:, j, i * P : (i + 1) * P], ident[:])
                 nc.vector.scalar_tensor_tensor(
                     out=exp_scores[:, i, cols],
                     in0=exp_scores[:, i, cols],
@@ -242,27 +224,30 @@ def tile_persistentgrucell_pc_kernel(
                 )
                 nc.sync.dma_start(out=out[i * P : (i + 1) * P, cols], in_=result[:, i, cols])
 
+        baddr_all = const.tile([P, SLOTS], BF16)
+        bforget_all = const.tile([P, SLOTS], BF16)
         start_block(0)
         finish_block(0)
-        spread_biases()
+        spread_over_partitions(baddr_row, baddr_all, nc.scalar.copy)
         start_block(1)
         finish_block(1)
+        spread_over_partitions(bforget_row, bforget_all, nc.scalar.copy)
+
+        bwrite_bank = psum.tile([P, P], BF16, tag="bank")
+        nc.tensor.transpose(bwrite_bank[:], bwrite_rows[:], ident_bf16[:])
+        nc.vector.tensor_copy(out=bwrite_cols[:], in_=bwrite_bank[:, 0:SLOT_TILES])
 
         for c in range(CHUNKS):
             addr_block = 2 * c
             forget_block = addr_block + 1
-            scores = scores_of(c, mx[addr_block])
+            scores = affine_of(c, mx[addr_block], baddr_all)
             start_block(addr_block + AHEAD)
-            finish_block(addr_block + AHEAD)
-            earlier_tanh_t = tanh_t if c > 0 else None
-            tanh_t = gate_pool.tile([P, ROW_TILES, BATCH], F32, tag="gate")
-            gate_tiles(tanh_t, 0, FORGET, c, mx[forget_block], ACT.Tanh, 0.5)
-            if c > 0:
-                keep_memory(c - 1, earlier_tanh_t)
-            gate_tiles(tanh_t, 1, FORGET, c, mx[forget_block], ACT.Tanh, 0.5)
-            start_block(forget_block + AHEAD)
             maxima_of(c, scores)
             exponentials_of(c, scores)
+            finish_block(addr_block + AHEAD)
+            forget = affine_of(c, mx[forget_block], bforget_all)
+            start_block(forget_block + AHEAD)
+            keep_memory(c, forget)
             finish_block(forget_block + AHEAD)
 
         small = [P, BATCH_TILES, CHUNKS]
@@ -291,14 +276,7 @@ def tile_persistentgrucell_pc_kernel(
 
         for c in range(CHUNKS):
             write_block = first_write_block + c
-            earlier_write_t = write_t if c > 0 else None
-            write_t = gate_pool.tile([P, ROW_TILES, BATCH], F32, tag="gate")
-            gate_tiles(write_t, 0, WRITE, c, mx[write_block], ACT.Sigmoid, 1.0)
-            if c > 0:
-                add_written(c - 1, earlier_write_t)
-            else:
-                keep_memory(CHUNKS - 1, tanh_t)
-            gate_tiles(write_t, 1, WRITE, c, mx[write_block], ACT.Sigmoid, 1.0)
+            write_t = write_chunk(c, mx[write_block])
             start_block(write_block + AHEAD)
+            add_written(c, write_t)
             finish_block(write_block + AHEAD)
-        add_written(CHUNKS - 1, write_t)

from contextlib import ExitStack

import concourse.mybir as mybir
from concourse.masks import make_identity

F32 = mybir.dt.float32
BF16 = mybir.dt.bfloat16
U32 = mybir.dt.uint32
U8 = mybir.dt.uint8
FP8X4 = mybir.dt.float8_e4m3fn_x4
ALU = mybir.AluOpType
ACT = mybir.ActivationFunctionType
AXIS = mybir.AxisListType

P = 128
BATCH = 512
HIDDEN = 1024
SLOTS = 2048
PACK = 4
PASSES = HIDDEN // (P * PACK)
PAIRS = 2
ROWS = 512
ROW_TILES = ROWS // P
ROW_WORDS = HIDDEN // 2
BATCH_TILES = BATCH // P
CHUNKS = SLOTS // ROWS
SLOT_TILES = SLOTS // P
RAW_BUFS = 4
AHEAD = 2

FLOPS = 2 * BATCH * HIDDEN * SLOTS * 3


def tile_persistentgrucell_pc_kernel(
    tc, hidden_new, persistent_memory, Waddr, baddr, Wwrite, bwrite, Wforget, bforget, out
):
    nc = tc.nc
    with ExitStack() as stack:
        stack.enter_context(tc.manual_schedule())
        const = stack.enter_context(tc.tile_pool(name="const", bufs=1))
        raw_pool = stack.enter_context(tc.tile_pool(name="raw", bufs=RAW_BUFS))
        grouped_pool = stack.enter_context(tc.tile_pool(name="grouped", bufs=2))
        mx_pool = stack.enter_context(tc.tile_pool(name="mx", bufs=4))
        affine_pool = stack.enter_context(tc.tile_pool(name="affine", bufs=3 * BATCH_TILES))
        gate_pool = stack.enter_context(tc.tile_pool(name="gate", bufs=2))
        psum = stack.enter_context(tc.psum_pool(name="psum", bufs=8))

        def chunk_rows(weight, c):
            return weight[c * ROWS : (c + 1) * ROWS, :]

        blocks = []
        for c in range(CHUNKS):
            blocks.extend([chunk_rows(Waddr, c), chunk_rows(Wforget, c)])
        first_write_block = len(blocks)
        blocks.extend([chunk_rows(Wwrite, c) for c in range(CHUNKS)])

        def load_rows(pool, rows):
            raw_rows = pool.tile([P, ROW_TILES * HIDDEN], BF16, tag="raw")
            for j in range(ROW_TILES):
                nc.sync.dma_start(out=raw_rows[:, j * HIDDEN : (j + 1) * HIDDEN], in_=rows[j * P : (j + 1) * P, :])
            return raw_rows

        ident = const.tile([P, P], F32)
        make_identity(nc, ident[:])
        ident_bf16 = const.tile([P, P], BF16)
        make_identity(nc, ident_bf16[:])
        ones = const.tile([P, P], BF16)
        nc.vector.memset(ones[:], 1.0)
        bwrite_rows = const.tile([P, P], BF16)
        nc.vector.memset(bwrite_rows[:], 0.0)
        baddr_row = const.tile([P, SLOTS], BF16)
        nc.vector.memset(baddr_row[:], 0.0)
        bforget_row = const.tile([P, SLOTS], BF16)
        nc.vector.memset(bforget_row[:], 0.0)

        hidden_raw = load_rows(const, hidden_new)
        raw = {0: load_rows(raw_pool, blocks[0])}
        nc.sync.dma_start(out=baddr_row[0:1, :], in_=baddr.rearrange("(o n) -> o n", o=1))
        nc.sync.dma_start(out=bforget_row[0:1, :], in_=bforget.rearrange("(o n) -> o n", o=1))
        nc.sync.dma_start(out=bwrite_rows[0:SLOT_TILES, :], in_=bwrite.rearrange("(t p) -> t p", p=P))
        for n in range(1, RAW_BUFS):
            raw[n] = load_rows(raw_pool, blocks[n])
        memory = const.tile([P, BATCH_TILES, SLOTS], BF16)
        nc.sync.dma_start(out=memory[:], in_=persistent_memory.rearrange("(i p) n -> p i n", p=P))

        def spread_over_partitions(bias_row, bias_all, copy_out):
            for c in range(CHUNKS):
                cols = slice(c * ROWS, (c + 1) * ROWS)
                bias_bank = psum.tile([P, ROWS], F32, tag="bank")
                nc.tensor.matmul(out=bias_bank[:], lhsT=ones[:], rhs=bias_row[:, cols], start=True, stop=True)
                copy_out(out=bias_all[:, cols], in_=bias_bank[:])

        def transpose_rows(raw_rows):
            words = raw_rows[:].bitcast(F32)
            grouped_rows = grouped_pool.tile([P, PASSES * ROWS * PACK], BF16, tag="grouped", align_bytes=64)
            grouped_words = grouped_rows[:].bitcast(F32).rearrange("p (g r u) -> p g r u", g=PASSES, u=PAIRS)
            for j in range(ROW_TILES):
                bank = psum.tile([P, PASSES * PAIRS, P], F32, tag="bank")
                for q in range(PASSES * PAIRS):
                    first = j * ROW_WORDS + q * P
                    nc.tensor.transpose(bank[:, q, :], words[:, first : first + P], ident[:])
                nc.scalar.copy(
                    out=grouped_words[:, :, j * P : (j + 1) * P, :],
                    in_=bank[:].rearrange("p (g u) r -> p g r u", u=PAIRS),
                )
            return grouped_rows

        def quantise(pool, grouped_rows):
            codes = pool.tile([P, PASSES * ROWS], U32, tag="codes", align_bytes=64)
            scales = pool.tile([P, PASSES * ROWS], U8, tag="scales", align_bytes=64)
            nc.vector.quantize_mx(out=codes[:].bitcast(FP8X4), scales=scales[:], in_=grouped_rows[:])
            return codes, scales

        grouped = {}
        mx = {}

        def start_block(n):
            if n < len(blocks):
                grouped[n] = transpose_rows(raw[n])
                if n + RAW_BUFS < len(blocks):
                    raw[n + RAW_BUFS] = load_rows(raw_pool, blocks[n + RAW_BUFS])

        def finish_block(n):
            if n < len(blocks):
                mx[n] = quantise(mx_pool, grouped[n])

        def mx_product(acc, stationary, tile_index, moving):
            for g in range(PASSES):
                s_cols = slice(g * ROWS + tile_index * P, g * ROWS + (tile_index + 1) * P)
                m_cols = slice(g * ROWS, (g + 1) * ROWS)
                nc.tensor.matmul_mx(
                    out=acc[:],
                    lhsT=stationary[0][:, s_cols].bitcast(FP8X4),
                    lhsT_scale=stationary[1][:, s_cols],
                    rhs=moving[0][:, m_cols].bitcast(FP8X4),
                    rhs_scale=moving[1][:, m_cols],
                    start=(g == 0),
                    stop=(g == PASSES - 1),
                )

        hidden_sum = const.tile([P, BATCH_TILES], F32)
        hidden_rows = hidden_raw[:].rearrange("p (i k) -> p i k", i=BATCH_TILES)
        half = BATCH_TILES // 2
        nc.vector.tensor_reduce(out=hidden_sum[:, 0:half], in_=hidden_rows[:, 0:half, :], axis=AXIS.X, op=ALU.add)
        hidden_mx = quantise(const, transpose_rows(hidden_raw))
        nc.vector.tensor_reduce(
            out=hidden_sum[:, half:BATCH_TILES], in_=hidden_rows[:, half:BATCH_TILES, :], axis=AXIS.X, op=ALU.add
        )

        def affine_of(c, weight_mx, bias_all):
            cols = slice(c * ROWS, (c + 1) * ROWS)
            tiles = []
            for i in range(BATCH_TILES):
                acc = psum.tile([P, ROWS], F32, tag="bank")
                mx_product(acc, hidden_mx, i, weight_mx)
                affine = affine_pool.tile([P, ROWS], F32, tag="affine")
                nc.vector.tensor_tensor(out=affine[:], in0=acc[:], in1=bias_all[:, cols], op=ALU.add)
                tiles.append(affine)
            return tiles

        exp_scores = const.tile([P, BATCH_TILES, SLOTS], F32)
        neg_max = const.tile([P, BATCH_TILES, CHUNKS], F32)
        exp_sum = const.tile([P, BATCH_TILES, CHUNKS], F32)

        def maxima_of(c, scores):
            for i in range(BATCH_TILES):
                nc.vector.tensor_reduce(
                    out=neg_max[:, i, c : c + 1], in_=scores[i][:], axis=AXIS.X, op=ALU.max, negate=True
                )

        def exponentials_of(c, scores):
            cols = slice(c * ROWS, (c + 1) * ROWS)
            for i in range(BATCH_TILES):
                nc.scalar.activation(
                    out=exp_scores[:, i, cols],
                    in_=scores[i][:],
                    func=ACT.Exp,
                    bias=neg_max[:, i, c : c + 1],
                    scale=1.0,
                    accum_out=exp_sum[:, i, c : c + 1],
                )

        result = const.tile([P, BATCH_TILES, SLOTS], F32)

        def keep_memory(c, forget):
            cols = slice(c * ROWS, (c + 1) * ROWS)
            for i in range(BATCH_TILES):
                nc.scalar.activation(out=forget[i][:], in_=forget[i][:], func=ACT.Tanh, scale=0.5)
                nc.gpsimd.tensor_scalar(
                    out=forget[i][:], in0=forget[i][:], scalar1=0.5, scalar2=0.5, op0=ALU.mult, op1=ALU.add
                )
                nc.gpsimd.tensor_tensor(out=result[:, i, cols], in0=forget[i][:], in1=memory[:, i, cols], op=ALU.mult)

        bwrite_cols = const.tile([P, SLOT_TILES], F32)

        def write_chunk(c, weight_mx):
            write_t = gate_pool.tile([P, ROW_TILES, BATCH], F32, tag="gate")
            for j in range(ROW_TILES):
                acc = psum.tile([P, BATCH], F32, tag="bank")
                mx_product(acc, weight_mx, j, hidden_mx)
                t = c * ROW_TILES + j
                nc.scalar.activation(
                    out=write_t[:, j, :], in_=acc[:], func=ACT.Sigmoid, bias=bwrite_cols[:, t : t + 1], scale=1.0
                )
            return write_t

        def add_written(c, write_t):
            cols = slice(c * ROWS, (c + 1) * ROWS)
            for i in range(BATCH_TILES):
                bank = psum.tile([P, ROWS], F32, tag="bank")
                for j in range(ROW_TILES):
                    nc.tensor.transpose(bank[:, j * P : (j + 1) * P], write_t[:, j, i * P : (i + 1) * P], ident[:])
                nc.vector.scalar_tensor_tensor(
                    out=exp_scores[:, i, cols],
                    in0=exp_scores[:, i, cols],
                    scalar=chunk_scale[:, i, c : c + 1],
                    in1=bank[:],
                    op0=ALU.mult,
                    op1=ALU.mult,
                )
                adder = (nc.gpsimd, nc.vector)[i % 2]
                adder.tensor_tensor(
                    out=result[:, i, cols], in0=result[:, i, cols], in1=exp_scores[:, i, cols], op=ALU.add
                )
                nc.sync.dma_start(out=out[i * P : (i + 1) * P, cols], in_=result[:, i, cols])

        baddr_all = const.tile([P, SLOTS], BF16)
        bforget_all = const.tile([P, SLOTS], BF16)
        start_block(0)
        finish_block(0)
        spread_over_partitions(baddr_row, baddr_all, nc.scalar.copy)
        start_block(1)
        finish_block(1)
        spread_over_partitions(bforget_row, bforget_all, nc.scalar.copy)

        bwrite_bank = psum.tile([P, P], BF16, tag="bank")
        nc.tensor.transpose(bwrite_bank[:], bwrite_rows[:], ident_bf16[:])
        nc.vector.tensor_copy(out=bwrite_cols[:], in_=bwrite_bank[:, 0:SLOT_TILES])

        for c in range(CHUNKS):
            addr_block = 2 * c
            forget_block = addr_block + 1
            scores = affine_of(c, mx[addr_block], baddr_all)
            start_block(addr_block + AHEAD)
            maxima_of(c, scores)
            exponentials_of(c, scores)
            finish_block(addr_block + AHEAD)
            forget = affine_of(c, mx[forget_block], bforget_all)
            start_block(forget_block + AHEAD)
            keep_memory(c, forget)
            finish_block(forget_block + AHEAD)

        small = [P, BATCH_TILES, CHUNKS]
        neg_top = const.tile([P, BATCH_TILES], F32)
        nc.vector.tensor_reduce(out=neg_top[:], in_=neg_max[:], axis=AXIS.X, op=ALU.min)
        below_top = const.tile(small, F32)
        nc.vector.tensor_tensor(
            out=below_top[:], in0=neg_top[:].unsqueeze(2).to_broadcast(small), in1=neg_max[:], op=ALU.subtract
        )
        rescale = const.tile(small, F32)
        nc.scalar.activation(out=rescale[:], in_=below_top[:], func=ACT.Exp)
        rescaled_sum = const.tile(small, F32)
        nc.vector.tensor_tensor(out=rescaled_sum[:], in0=rescale[:], in1=exp_sum[:], op=ALU.mult)
        row_sum = const.tile([P, BATCH_TILES], F32)
        nc.vector.tensor_reduce(out=row_sum[:], in_=rescaled_sum[:], axis=AXIS.X, op=ALU.add)
        inv_row_sum = const.tile([P, BATCH_TILES], F32)
        nc.vector.reciprocal(out=inv_row_sum[:], in_=row_sum[:])
        row_scale = const.tile([P, BATCH_TILES], F32)
        nc.vector.scalar_tensor_tensor(
            out=row_scale[:], in0=hidden_sum[:], scalar=1.0 / HIDDEN, in1=inv_row_sum[:], op0=ALU.mult, op1=ALU.mult
        )
        chunk_scale = const.tile(small, F32)
        nc.vector.tensor_tensor(
            out=chunk_scale[:], in0=rescale[:], in1=row_scale[:].unsqueeze(2).to_broadcast(small), op=ALU.mult
        )

        for c in range(CHUNKS):
            write_block = first_write_block + c
            write_t = write_chunk(c, mx[write_block])
            start_block(write_block + AHEAD)
            add_written(c, write_t)
            finish_block(write_block + AHEAD)
